import numpy as np
import ml_dtypes


def mxq(x, axis, fmt="e4m3"):
    dtype, down = {"e4m3": (ml_dtypes.float8_e4m3fn, 7), "e5m2": (ml_dtypes.float8_e5m2, 14)}[fmt]
    v = np.moveaxis(np.asarray(x, np.float32).astype(ml_dtypes.bfloat16).astype(np.float64), axis, -1)
    blocks = v.reshape(v.shape[:-1] + (-1, 32))
    amax = np.abs(blocks).max(-1, keepdims=True)
    byte = np.maximum(np.where(amax > 0, np.frexp(amax)[1] - 1 + 127, 0) - down, 1)
    scale = np.exp2(byte - 127.0)
    codes = (blocks / scale).astype(np.float32).astype(dtype).astype(np.float64)
    return np.moveaxis((codes * scale).reshape(v.shape), -1, axis)


WIDE = False


def mx_kscale(k):
    if not WIDE:
        return np.ones(k)
    levels = np.array([10, -10, 5, -5, 0])
    a = np.random.permutation(np.resize(levels, k // 512 * 4)).reshape(k // 512, 4)
    idx = np.arange(k)
    return np.exp2(a[idx // 512, idx % 128 // 32])


BF16 = ml_dtypes.bfloat16


def bf(x):
    return np.asarray(x, np.float32).astype(BF16)


def f64(x):
    return np.asarray(x).astype(np.float64)


B, S, HID, NH, HD, RD, RATIO = 4, 4096, 512, 8, 64, 32, 4
THETA = 10000.0
NW = S // RATIO
HALF = RD // 2


def rope_tables(positions):
    inv_freq = 1.0 / THETA ** (np.arange(HALF) / HALF)
    ang = positions[:, None] * inv_freq[None, :]
    return np.cos(ang), np.sin(ang)


def rope_interleaved(x, cos, sin):
    nope, rope = x[..., :-RD], x[..., -RD:]
    pr = rope.reshape(rope.shape[:-1] + (HALF, 2))
    a, b = pr[..., 0], pr[..., 1]
    new = np.stack([a * cos - b * sin, a * sin + b * cos], axis=-1).reshape(rope.shape)
    return np.concatenate([nope, new], axis=-1)


def remap(t, fill):
    cur = t[..., HD:]
    prev = np.concatenate([np.full((B, 1, RATIO, HD), fill), t[:, :-1, :, :HD]], axis=1)
    return np.concatenate([prev, cur], axis=2)


def pool_overlap(kv, gate, ape):
    kv_o = remap(kv.reshape(B, NW, RATIO, 2 * HD), 0.0)
    gate_o = remap(gate.reshape(B, NW, RATIO, 2 * HD) + ape, -np.inf)
    e = np.exp(gate_o - gate_o.max(axis=2, keepdims=True))
    w = e / e.sum(axis=2, keepdims=True)
    return (kv_o * w).sum(axis=2)


def setup_inputs():
    s = mx_kscale(HID)
    return {"hidden": bf(np.random.standard_normal((B, S, HID)) * s),
            "wkv": bf(np.random.standard_normal((HID, 2 * HD)) * 2.0 / np.sqrt(HID) / s[:, None]),
            "wgate": bf(np.random.standard_normal((HID, 2 * HD)) / np.sqrt(HID) / s[:, None]),
            "ape": bf(np.random.standard_normal((RATIO, 2 * HD)) * 0.5)}


def reference(hidden, wkv, wgate, ape):
    hq = mxq(f64(hidden), 2, "e4m3")
    kv = hq @ mxq(f64(wkv), 0, "e4m3")
    gate = hq @ mxq(f64(wgate), 0, "e4m3")
    pooled = pool_overlap(kv, gate, f64(ape))
    ck, sk = rope_tables(np.arange(NW) * RATIO)
    k_rot = rope_interleaved(pooled, ck, sk)
    return k_rot, pooled

@@ -1,0 +1,311 @@
+from contextlib import ExitStack
+import math
+
+import concourse.mybir as mybir
+from concourse.masks import make_identity
+
+F32 = mybir.dt.float32
+BF16 = mybir.dt.bfloat16
+I32 = mybir.dt.int32
+U32 = mybir.dt.uint32
+U8 = mybir.dt.uint8
+FP8X4 = mybir.dt.float8_e4m3fn_x4
+ALU = mybir.AluOpType
+ACT = mybir.ActivationFunctionType
+AXIS = mybir.AxisListType
+
+P = 128
+BATCH, SEQ, HID = 4, 4096, 512
+RATIO = 4
+HD = 64
+FEAT = 2 * HD
+ROPE = 32
+PAIRS = ROPE // 2
+THETA = 10000.0
+WPP = SEQ // RATIO // P
+WORDS = HID // 2
+GROUP = 4
+NEXT, THIS = 0, 1
+MINUS_BIG = -1.0e30
+ROUND_MAGIC = 1.5 * 2.0**23
+
+FLOPS = 2 * BATCH * SEQ * HID * 2 * FEAT
+
+
+def leading_bits(x, bits):
+    if x == 0.0:
+        return 0.0
+    step = 1.0
+    while abs(x) / step >= 2.0**bits:
+        step *= 2.0
+    while abs(x) / step < 2.0 ** (bits - 1):
+        step /= 2.0
+    return round(x / step) * step
+
+
+def quantise_weights(nc, const, wgate, wkv):
+    raw = const.tile([P, 4, 2 * FEAT], BF16)
+    for w, first in ((wgate, 0), (wkv, FEAT)):
+        for u in range(2):
+            nc.scalar.dma_start(
+                out=raw[:, 2 * u : 2 * u + 2, first : first + FEAT],
+                in_=w[WORDS * u : WORDS * (u + 1), :].rearrange("(q e) c -> q e c", e=2),
+            )
+    grouped = const.tile([P, 2 * FEAT, 4], BF16, align_bytes=64)
+    nc.vector.tensor_copy(out=grouped[:], in_=raw[:].rearrange("q t c -> q c t"))
+    w_codes = const.tile([P, 2 * FEAT], U32, align_bytes=64)
+    w_scales = const.tile([P, 2 * FEAT], U8, align_bytes=64)
+    nc.vector.quantize_mx(
+        out=w_codes[:].bitcast(FP8X4),
+        scales=w_scales[:],
+        in_=grouped[:].rearrange("q c t -> q (c t)"),
+    )
+    return w_codes, w_scales
+
+
+def rope_table(nc, const):
+    position_int = const.tile([P, WPP], I32)
+    nc.gpsimd.iota(position_int[:], pattern=[[RATIO, WPP]], base=0, channel_multiplier=RATIO * WPP)
+    position = const.tile([P, WPP], F32)
+    nc.vector.tensor_copy(out=position[:], in_=position_int[:])
+
+    angle_hi = const.tile([P, WPP, PAIRS], F32)
+    angle_lo = const.tile([P, WPP, PAIRS], F32)
+    for j in range(PAIRS):
+        frequency = 1.0 / THETA ** (j / PAIRS)
+        leading = leading_bits(frequency, 12)
+        for angle, factor in ((angle_hi, leading), (angle_lo, frequency - leading)):
+            nc.gpsimd.tensor_scalar(
+                out=angle[:, :, j], in0=position[:], scalar1=factor, scalar2=0.0,
+                op0=ALU.mult, op1=ALU.add,
+            )
+
+    turns = const.tile([P, WPP, PAIRS], F32)
+    nc.gpsimd.tensor_tensor(out=turns[:], in0=angle_hi[:], in1=angle_lo[:], op=ALU.add)
+    nc.gpsimd.tensor_scalar(
+        out=turns[:], in0=turns[:], scalar1=1.0 / (2.0 * math.pi), scalar2=ROUND_MAGIC,
+        op0=ALU.mult, op1=ALU.add,
+    )
+    nc.gpsimd.tensor_single_scalar(out=turns[:], in_=turns[:], scalar=ROUND_MAGIC, op=ALU.subtract)
+
+    piece_1 = leading_bits(2.0 * math.pi, 12)
+    piece_2 = leading_bits(2.0 * math.pi - piece_1, 12)
+    piece_3 = 2.0 * math.pi - piece_1 - piece_2
+    rest = const.tile([P, WPP, PAIRS], F32)
+    product = const.tile([P, WPP, PAIRS], F32)
+    nc.gpsimd.tensor_scalar(
+        out=product[:], in0=turns[:], scalar1=-piece_1, scalar2=0.0, op0=ALU.mult, op1=ALU.add
+    )
+    nc.gpsimd.tensor_tensor(out=rest[:], in0=angle_hi[:], in1=product[:], op=ALU.add)
+    nc.gpsimd.tensor_scalar(
+        out=product[:], in0=turns[:], scalar1=-piece_2, scalar2=0.0, op0=ALU.mult, op1=ALU.add
+    )
+    nc.gpsimd.tensor_tensor(out=rest[:], in0=rest[:], in1=product[:], op=ALU.add)
+    nc.gpsimd.tensor_tensor(out=rest[:], in0=rest[:], in1=angle_lo[:], op=ALU.add)
+    nc.gpsimd.tensor_scalar(
+        out=product[:], in0=turns[:], scalar1=-piece_3, scalar2=0.0, op0=ALU.mult, op1=ALU.add
+    )
+    nc.gpsimd.tensor_tensor(out=rest[:], in0=rest[:], in1=product[:], op=ALU.add)
+
+    sin_half = const.tile([P, WPP, PAIRS], F32)
+    sin_quarter = const.tile([P, WPP, PAIRS], F32)
+    nc.scalar.activation(out=sin_half[:], in_=rest[:], func=ACT.Sin, scale=0.5)
+    nc.scalar.activation(out=sin_quarter[:], in_=rest[:], func=ACT.Sin, scale=0.25)
+    cos_half = const.tile([P, WPP, PAIRS], F32)
+    nc.gpsimd.tensor_tensor(out=cos_half[:], in0=sin_quarter[:], in1=sin_quarter[:], op=ALU.mult)
+    nc.gpsimd.tensor_scalar(
+        out=cos_half[:], in0=cos_half[:], scalar1=-2.0, scalar2=1.0, op0=ALU.mult, op1=ALU.add
+    )
+    half_of_sin = const.tile([P, WPP, PAIRS], F32)
+    nc.gpsimd.tensor_tensor(out=half_of_sin[:], in0=sin_half[:], in1=cos_half[:], op=ALU.mult)
+    square = const.tile([P, WPP, PAIRS], F32)
+    nc.gpsimd.tensor_tensor(out=square[:], in0=sin_half[:], in1=sin_half[:], op=ALU.mult)
+
+    table = const.tile([P, WPP, 2, PAIRS, 2], F32)
+    for row, column in ((0, 0), (1, 1)):
+        nc.gpsimd.tensor_scalar(
+            out=table[:, :, row, :, column], in0=square[:], scalar1=-2.0, scalar2=1.0,
+            op0=ALU.mult, op1=ALU.add,
+        )
+    for row, column, sign in ((0, 1, -2.0), (1, 0, 2.0)):
+        nc.gpsimd.tensor_scalar(
+            out=table[:, :, row, :, column], in0=half_of_sin[:], scalar1=sign, scalar2=0.0,
+            op0=ALU.mult, op1=ALU.add,
+        )
+    return table
+
+
+def tile_deepseekv4attention_pa_t_kernel(tc, hidden, wkv, wgate, ape, out_0, out_1):
+    nc = tc.nc
+    with ExitStack() as ctx:
+        const = ctx.enter_context(tc.tile_pool(name="const", bufs=1))
+        tokens = ctx.enter_context(tc.tile_pool(name="tokens", bufs=6))
+        operand = ctx.enter_context(tc.tile_pool(name="operand", bufs=3))
+        sequence = ctx.enter_context(tc.tile_pool(name="sequence", bufs=2))
+        work = ctx.enter_context(tc.tile_pool(name="work", bufs=2))
+        psum_words = ctx.enter_context(tc.psum_pool(name="psum_words", bufs=3))
+        psum_proj = ctx.enter_context(tc.psum_pool(name="psum_proj", bufs=2))
+        psum_shift = ctx.enter_context(tc.psum_pool(name="psum_shift", bufs=1))
+
+        w_codes, w_scales = quantise_weights(nc, const, wgate, wkv)
+
+        ape_bf16 = const.tile([P, RATIO * FEAT], BF16)
+        nc.scalar.dma_start(
+            out=ape_bf16[:], in_=ape.rearrange("r c -> (r c)").partition_broadcast(P)
+        )
+        ape_f32 = const.tile([P, RATIO * FEAT], F32)
+        nc.vector.tensor_copy(out=ape_f32[:], in_=ape_bf16[:])
+
+        identity = const.tile([P, P], F32)
+        make_identity(nc, identity[:])
+        padded = const.tile([P, P + 1], F32)
+        nc.gpsimd.memset(padded[:, 0:1], 0.0)
+        make_identity(nc, padded[:, 1 : P + 1])
+        down = padded[:, 0:P]
+        no_window_before = const.tile([P, 1], F32)
+        nc.vector.tensor_scalar(
+            out=no_window_before[:], in0=identity[:, 0:1], scalar1=MINUS_BIG, scalar2=None,
+            op0=ALU.mult,
+        )
+
+        table = rope_table(nc, const)
+
+        def project(b, j, gates, values):
+            x = tokens.tile([P, RATIO * HID], BF16)
+            nc.sync.dma_start(
+                out=x[:],
+                in_=hidden[b].rearrange("(p t) k -> p (t k)", t=RATIO * WPP)[
+                    :, j * RATIO * HID : (j + 1) * RATIO * HID
+                ],
+            )
+            x_words = x[:].bitcast(F32)
+            grouped = operand.tile([P, RATIO * P, 4], BF16, align_bytes=64)
+            grouped_words = grouped[:].bitcast(F32)
+            for pair in range(RATIO // 2):
+                planes = psum_words.tile([P, 2, 2 * P], F32)
+                for r in (2 * pair, 2 * pair + 1):
+                    for u in range(2):
+                        nc.tensor.transpose(
+                            planes[:, u, (r % 2) * P : (r % 2 + 1) * P],
+                            x_words[:, r * WORDS + u * P : r * WORDS + (u + 1) * P],
+                            identity[:],
+                        )
+                nc.scalar.copy(
+                    out=grouped_words[:, 2 * pair * P : 2 * (pair + 1) * P, :],
+                    in_=planes[:].rearrange("q u c -> q c u"),
+                )
+            codes = operand.tile([P, RATIO * P], U32, align_bytes=64)
+            scales = operand.tile([P, RATIO * P], U8, align_bytes=64)
+            nc.vector.quantize_mx(
+                out=codes[:].bitcast(FP8X4),
+                scales=scales[:],
+                in_=grouped[:].rearrange("q c t -> q (c t)"),
+            )
+            gate_psum = psum_proj.tile([P, RATIO, FEAT], F32)
+            kv_psum = psum_proj.tile([P, RATIO, FEAT], F32)
+            for r in range(RATIO):
+                for psum, first in ((gate_psum, 0), (kv_psum, FEAT)):
+                    nc.tensor.matmul_mx(
+                        out=psum[:, r, :],
+                        lhsT=codes[:, r * P : (r + 1) * P].bitcast(FP8X4),
+                        lhsT_scale=scales[:, r * P : (r + 1) * P],
+                        rhs=w_codes[:, first : first + FEAT].bitcast(FP8X4),
+                        rhs_scale=w_scales[:, first : first + FEAT],
+                        start=True,
+                        stop=True,
+                    )
+            nc.vector.tensor_tensor(
+                out=gates[:, j + 1].rearrange("p r h f -> p (r h f)"),
+                in0=gate_psum[:].rearrange("p r c -> p (r c)"),
+                in1=ape_f32[:],
+                op=ALU.add,
+            )
+            nc.scalar.copy(
+                out=values[:, j + 1].rearrange("p r h f -> p (r h f)"),
+                in_=kv_psum[:].rearrange("p r c -> p (r c)"),
+            )
+
+        def hand_down(gates, values):
+            moved = psum_shift.tile([P, 2, RATIO, HD], F32)
+            nc.tensor.matmul(
+                out=moved[:, 0], lhsT=down, rhs=gates[:, WPP, :, NEXT, :], start=True, stop=True
+            )
+            nc.tensor.matmul(
+                out=moved[:, 1], lhsT=down, rhs=values[:, WPP, :, NEXT, :], start=True, stop=True
+            )
+            nc.vector.tensor_scalar(
+                out=gates[:, 0, :, NEXT, :], in0=moved[:, 0], scalar1=no_window_before[:, 0:1],
+                scalar2=None, op0=ALU.add,
+            )
+            nc.scalar.copy(out=values[:, 0, :, NEXT, :], in_=moved[:, 1])
+
+        def pool_windows(b, first, gates, values):
+            last = first + GROUP
+            halves = (
+                (gates[:, first + 1 : last + 1, :, THIS, :], values[:, first + 1 : last + 1, :, THIS, :]),
+                (gates[:, first:last, :, NEXT, :], values[:, first:last, :, NEXT, :]),
+            )
+            top_4 = work.tile([P, GROUP, RATIO, HD], F32)
+            nc.vector.tensor_tensor(out=top_4[:], in0=halves[0][0], in1=halves[1][0], op=ALU.max)
+            top_2 = work.tile([P, GROUP, 2, HD], F32)
+            nc.vector.tensor_tensor(
+                out=top_2[:], in0=top_4[:, :, 0:2, :], in1=top_4[:, :, 2:4, :], op=ALU.max
+            )
+            top = work.tile([P, GROUP, HD], F32)
+            nc.vector.tensor_tensor(out=top[:], in0=top_2[:, :, 0, :], in1=top_2[:, :, 1, :], op=ALU.max)
+            for g, v in halves:
+                nc.vector.tensor_tensor(
+                    out=g, in0=g, in1=top[:].unsqueeze(2).to_broadcast([P, GROUP, RATIO, HD]),
+                    op=ALU.subtract,
+                )
+                nc.scalar.activation(out=g, in_=g, func=ACT.Exp)
+            for g, v in halves:
+                nc.vector.tensor_tensor(out=v, in0=v, in1=g, op=ALU.mult)
+            sums_4 = work.tile([P, 2, GROUP, RATIO, HD], F32)
+            for which in range(2):
+                nc.vector.tensor_tensor(
+                    out=sums_4[:, which], in0=halves[0][which], in1=halves[1][which], op=ALU.add
+                )
+            sums_2 = work.tile([P, 2, GROUP, 2, HD], F32)
+            nc.vector.tensor_tensor(
+                out=sums_2[:], in0=sums_4[:, :, :, 0:2, :], in1=sums_4[:, :, :, 2:4, :], op=ALU.add
+            )
+            sums = work.tile([P, 2, GROUP, HD], F32)
+            nc.vector.tensor_tensor(
+                out=sums[:], in0=sums_2[:, :, :, 0, :], in1=sums_2[:, :, :, 1, :], op=ALU.add
+            )
+            inverse = work.tile([P, GROUP, HD], F32)
+            nc.vector.reciprocal(out=inverse[:], in_=sums[:, 0])
+            pooled = work.tile([P, GROUP, HD], F32)
+            nc.vector.tensor_tensor(out=pooled[:], in0=sums[:, 1], in1=inverse[:], op=ALU.mult)
+
+            products = work.tile([P, GROUP, 2, ROPE], F32)
+            nc.vector.tensor_tensor(
+                out=products[:],
+                in0=pooled[:, :, HD - ROPE : HD].unsqueeze(2).to_broadcast([P, GROUP, 2, ROPE]),
+                in1=table[:, first:last].rearrange("p w o j i -> p w o (j i)"),
+                op=ALU.mult,
+            )
+            rotated = work.tile([P, GROUP, HD], F32)
+            nc.vector.tensor_reduce(
+                out=rotated[:, :, HD - ROPE : HD].rearrange("p w (j o) -> p w o j", o=2),
+                in_=products[:].rearrange("p w o (j i) -> p w o j i", i=2),
+                axis=AXIS.X,
+                op=ALU.add,
+            )
+            nc.scalar.copy(out=rotated[:, :, 0 : HD - ROPE], in_=pooled[:, :, 0 : HD - ROPE])
+            for out, result in ((out_0, rotated), (out_1, pooled)):
+                nc.sync.dma_start(
+                    out=out[b].rearrange("(p w) f -> p w f", w=WPP)[:, first:last, :], in_=result[:]
+                )
+
+        for b in range(BATCH):
+            gates = sequence.tile([P, WPP + 1, RATIO, 2, HD], F32)
+            values = sequence.tile([P, WPP + 1, RATIO, 2, HD], F32)
+            project(b, WPP - 1, gates, values)
+            hand_down(gates, values)
+            for j in range(WPP - 1):
+                project(b, j, gates, values)
+                if (j + 1) % GROUP == 0:
+                    pool_windows(b, j + 1 - GROUP, gates, values)
+            pool_windows(b, WPP - GROUP, gates, values)

@@ -25,7 +25,12 @@ THETA = 10000.0
 WPP = SEQ // RATIO // P
 WORDS = HID // 2
 GROUP = 4
-NEXT, THIS = 0, 1
+UNITS = BATCH * WPP
+GROUPS = UNITS // GROUP
+LOADS_AHEAD = 7
+FLIPS_AHEAD = 3
+SLOTS = 2 * RATIO
+HALF = RATIO * HD
 MINUS_BIG = -1.0e30
 ROUND_MAGIC = 1.5 * 2.0**23
 
@@ -44,26 +49,30 @@ def leading_bits(x, bits):
 
 
 def quantise_weights(nc, const, wgate, wkv):
-    raw = const.tile([P, 4, 2 * FEAT], BF16)
-    for w, first in ((wgate, 0), (wkv, FEAT)):
+    raw = const.tile([P, 4, 2, FEAT], BF16)
+    for m, w in enumerate((wgate, wkv)):
         for u in range(2):
-            nc.scalar.dma_start(
-                out=raw[:, 2 * u : 2 * u + 2, first : first + FEAT],
+            nc.sync.dma_start(
+                out=raw[:, 2 * u : 2 * u + 2, m, :],
                 in_=w[WORDS * u : WORDS * (u + 1), :].rearrange("(q e) c -> q e c", e=2),
             )
-    grouped = const.tile([P, 2 * FEAT, 4], BF16, align_bytes=64)
-    nc.vector.tensor_copy(out=grouped[:], in_=raw[:].rearrange("q t c -> q c t"))
+    grouped = const.tile([P, 2, 2, HD, 4], BF16, align_bytes=64)
+    for a in range(2):
+        nc.vector.tensor_copy(
+            out=grouped[:, :, 1 - a, :, :],
+            in_=raw[:, :, :, a * HD : (a + 1) * HD].rearrange("q t m f -> q m f t"),
+        )
     w_codes = const.tile([P, 2 * FEAT], U32, align_bytes=64)
     w_scales = const.tile([P, 2 * FEAT], U8, align_bytes=64)
     nc.vector.quantize_mx(
         out=w_codes[:].bitcast(FP8X4),
         scales=w_scales[:],
-        in_=grouped[:].rearrange("q c t -> q (c t)"),
+        in_=grouped[:].rearrange("q m a f t -> q (m a f t)"),
     )
     return w_codes, w_scales
 
 
-def rope_table(nc, const):
+def rope_angles(nc, const):
     position_int = const.tile([P, WPP], I32)
     nc.gpsimd.iota(position_int[:], pattern=[[RATIO, WPP]], base=0, channel_multiplier=RATIO * WPP)
     position = const.tile([P, WPP], F32)
@@ -75,38 +84,38 @@ def rope_table(nc, const):
         frequency = 1.0 / THETA ** (j / PAIRS)
         leading = leading_bits(frequency, 12)
         for angle, factor in ((angle_hi, leading), (angle_lo, frequency - leading)):
-            nc.gpsimd.tensor_scalar(
-                out=angle[:, :, j], in0=position[:], scalar1=factor, scalar2=0.0,
-                op0=ALU.mult, op1=ALU.add,
+            nc.vector.tensor_scalar(
+                out=angle[:, :, j], in0=position[:], scalar1=factor, scalar2=None, op0=ALU.mult
             )
 
     turns = const.tile([P, WPP, PAIRS], F32)
-    nc.gpsimd.tensor_tensor(out=turns[:], in0=angle_hi[:], in1=angle_lo[:], op=ALU.add)
-    nc.gpsimd.tensor_scalar(
+    nc.vector.tensor_tensor(out=turns[:], in0=angle_hi[:], in1=angle_lo[:], op=ALU.add)
+    nc.vector.tensor_scalar(
         out=turns[:], in0=turns[:], scalar1=1.0 / (2.0 * math.pi), scalar2=ROUND_MAGIC,
         op0=ALU.mult, op1=ALU.add,
     )
-    nc.gpsimd.tensor_single_scalar(out=turns[:], in_=turns[:], scalar=ROUND_MAGIC, op=ALU.subtract)
+    nc.vector.tensor_scalar(
+        out=turns[:], in0=turns[:], scalar1=ROUND_MAGIC, scalar2=None, op0=ALU.subtract
+    )
 
     piece_1 = leading_bits(2.0 * math.pi, 12)
     piece_2 = leading_bits(2.0 * math.pi - piece_1, 12)
     piece_3 = 2.0 * math.pi - piece_1 - piece_2
     rest = const.tile([P, WPP, PAIRS], F32)
-    product = const.tile([P, WPP, PAIRS], F32)
-    nc.gpsimd.tensor_scalar(
-        out=product[:], in0=turns[:], scalar1=-piece_1, scalar2=0.0, op0=ALU.mult, op1=ALU.add
+    nc.vector.scalar_tensor_tensor(
+        out=rest[:], in0=turns[:], scalar=-piece_1, in1=angle_hi[:], op0=ALU.mult, op1=ALU.add
     )
-    nc.gpsimd.tensor_tensor(out=rest[:], in0=angle_hi[:], in1=product[:], op=ALU.add)
-    nc.gpsimd.tensor_scalar(
-        out=product[:], in0=turns[:], scalar1=-piece_2, scalar2=0.0, op0=ALU.mult, op1=ALU.add
+    nc.vector.scalar_tensor_tensor(
+        out=rest[:], in0=turns[:], scalar=-piece_2, in1=rest[:], op0=ALU.mult, op1=ALU.add
     )
-    nc.gpsimd.tensor_tensor(out=rest[:], in0=rest[:], in1=product[:], op=ALU.add)
-    nc.gpsimd.tensor_tensor(out=rest[:], in0=rest[:], in1=angle_lo[:], op=ALU.add)
-    nc.gpsimd.tensor_scalar(
-        out=product[:], in0=turns[:], scalar1=-piece_3, scalar2=0.0, op0=ALU.mult, op1=ALU.add
+    nc.vector.tensor_tensor(out=rest[:], in0=rest[:], in1=angle_lo[:], op=ALU.add)
+    nc.vector.scalar_tensor_tensor(
+        out=rest[:], in0=turns[:], scalar=-piece_3, in1=rest[:], op0=ALU.mult, op1=ALU.add
     )
-    nc.gpsimd.tensor_tensor(out=rest[:], in0=rest[:], in1=product[:], op=ALU.add)
+    return rest
 
+
+def rope_table(nc, const, rest):
     sin_half = const.tile([P, WPP, PAIRS], F32)
     sin_quarter = const.tile([P, WPP, PAIRS], F32)
     nc.scalar.activation(out=sin_half[:], in_=rest[:], func=ACT.Sin, scale=0.5)
@@ -139,25 +148,33 @@ def tile_deepseekv4attention_pa_t_kernel(tc, hidden, wkv, wgate, ape, out_0, out
     nc = tc.nc
     with ExitStack() as ctx:
         const = ctx.enter_context(tc.tile_pool(name="const", bufs=1))
-        tokens = ctx.enter_context(tc.tile_pool(name="tokens", bufs=6))
-        operand = ctx.enter_context(tc.tile_pool(name="operand", bufs=3))
+        tokens = ctx.enter_context(tc.tile_pool(name="tokens", bufs=LOADS_AHEAD - FLIPS_AHEAD + 1))
+        words = ctx.enter_context(tc.tile_pool(name="words", bufs=FLIPS_AHEAD + 1))
+        operand = ctx.enter_context(tc.tile_pool(name="operand", bufs=2))
         sequence = ctx.enter_context(tc.tile_pool(name="sequence", bufs=2))
         work = ctx.enter_context(tc.tile_pool(name="work", bufs=2))
-        psum_words = ctx.enter_context(tc.psum_pool(name="psum_words", bufs=3))
+        psum_words = ctx.enter_context(tc.psum_pool(name="psum_words", bufs=2))
         psum_proj = ctx.enter_context(tc.psum_pool(name="psum_proj", bufs=2))
-        psum_shift = ctx.enter_context(tc.psum_pool(name="psum_shift", bufs=1))
+        psum_sums = ctx.enter_context(tc.psum_pool(name="psum_sums", bufs=1))
 
+        rest = rope_angles(nc, const)
         w_codes, w_scales = quantise_weights(nc, const, wgate, wkv)
 
-        ape_bf16 = const.tile([P, RATIO * FEAT], BF16)
-        nc.scalar.dma_start(
-            out=ape_bf16[:], in_=ape.rearrange("r c -> (r c)").partition_broadcast(P)
+        ape_bf16 = const.tile([P, RATIO, FEAT], BF16)
+        nc.sync.dma_start(
+            out=ape_bf16[:].rearrange("p r c -> p (r c)"),
+            in_=ape.rearrange("r c -> (r c)").partition_broadcast(P),
         )
-        ape_f32 = const.tile([P, RATIO * FEAT], F32)
-        nc.vector.tensor_copy(out=ape_f32[:], in_=ape_bf16[:])
+        ape_f32 = const.tile([P, RATIO, 2, HD], F32)
+        for a in range(2):
+            nc.vector.tensor_copy(out=ape_f32[:, :, 1 - a, :], in_=ape_bf16[:, :, a * HD : (a + 1) * HD])
 
         identity = const.tile([P, P], F32)
         make_identity(nc, identity[:])
+        both_parities = const.tile([P, HD], F32)
+        nc.vector.tensor_tensor(
+            out=both_parities[:], in0=identity[:, 0:HD], in1=identity[:, HD:P], op=ALU.add
+        )
         padded = const.tile([P, P + 1], F32)
         nc.gpsimd.memset(padded[:, 0:1], 0.0)
         make_identity(nc, padded[:, 1 : P + 1])
@@ -168,18 +185,23 @@ def tile_deepseekv4attention_pa_t_kernel(tc, hidden, wkv, wgate, ape, out_0, out
             op0=ALU.mult,
         )
 
-        table = rope_table(nc, const)
+        loaded, grouped_words_of, operand_of, products_of, tapes = {}, {}, {}, {}, {}
+        moved_of, flipped_of, sums_of, table_of = {}, {}, {}, {}
 
-        def project(b, j, gates, values):
+        def load(g):
+            j = (g - 1) % WPP
             x = tokens.tile([P, RATIO * HID], BF16)
             nc.sync.dma_start(
                 out=x[:],
-                in_=hidden[b].rearrange("(p t) k -> p (t k)", t=RATIO * WPP)[
+                in_=hidden[g // WPP].rearrange("(p t) k -> p (t k)", t=RATIO * WPP)[
                     :, j * RATIO * HID : (j + 1) * RATIO * HID
                 ],
             )
-            x_words = x[:].bitcast(F32)
-            grouped = operand.tile([P, RATIO * P, 4], BF16, align_bytes=64)
+            loaded[g] = x
+
+        def flip_words(g):
+            x_words = loaded[g][:].bitcast(F32)
+            grouped = words.tile([P, RATIO * P, 4], BF16, align_bytes=64)
             grouped_words = grouped[:].bitcast(F32)
             for pair in range(RATIO // 2):
                 planes = psum_words.tile([P, 2, 2 * P], F32)
@@ -194,19 +216,26 @@ def tile_deepseekv4attention_pa_t_kernel(tc, hidden, wkv, wgate, ape, out_0, out
                     out=grouped_words[:, 2 * pair * P : 2 * (pair + 1) * P, :],
                     in_=planes[:].rearrange("q u c -> q c u"),
                 )
+            grouped_words_of[g] = grouped
+
+        def quantise(g):
             codes = operand.tile([P, RATIO * P], U32, align_bytes=64)
             scales = operand.tile([P, RATIO * P], U8, align_bytes=64)
             nc.vector.quantize_mx(
                 out=codes[:].bitcast(FP8X4),
                 scales=scales[:],
-                in_=grouped[:].rearrange("q c t -> q (c t)"),
+                in_=grouped_words_of[g][:].rearrange("q c t -> q (c t)"),
             )
-            gate_psum = psum_proj.tile([P, RATIO, FEAT], F32)
-            kv_psum = psum_proj.tile([P, RATIO, FEAT], F32)
+            operand_of[g] = (codes, scales)
+
+        def project(g):
+            codes, scales = operand_of[g]
+            gate_psum = psum_proj.tile([P, RATIO, 2, HD], F32)
+            kv_psum = psum_proj.tile([P, RATIO, 2, HD], F32)
             for r in range(RATIO):
                 for psum, first in ((gate_psum, 0), (kv_psum, FEAT)):
                     nc.tensor.matmul_mx(
-                        out=psum[:, r, :],
+                        out=psum[:, r].rearrange("p a f -> p (a f)"),
                         lhsT=codes[:, r * P : (r + 1) * P].bitcast(FP8X4),
                         lhsT_scale=scales[:, r * P : (r + 1) * P],
                         rhs=w_codes[:, first : first + FEAT].bitcast(FP8X4),
@@ -214,98 +243,167 @@ def tile_deepseekv4attention_pa_t_kernel(tc, hidden, wkv, wgate, ape, out_0, out
                         start=True,
                         stop=True,
                     )
+            products_of[g] = (gate_psum, kv_psum)
+
+        def land(g):
+            if g % WPP == 0:
+                gates = sequence.tile([P, (2 * WPP + 1) * HALF], F32)
+                values = sequence.tile([P, (2 * WPP + 1) * HALF], F32)
+                tapes[g // WPP] = (gates, values)
+            gates, values = tapes[g // WPP]
+            gate_psum, kv_psum = products_of[g]
+            j = (g - 1) % WPP
+            run = slice(HALF + j * 2 * HALF, HALF + (j + 1) * 2 * HALF)
             nc.vector.tensor_tensor(
-                out=gates[:, j + 1].rearrange("p r h f -> p (r h f)"),
-                in0=gate_psum[:].rearrange("p r c -> p (r c)"),
-                in1=ape_f32[:],
+                out=gates[:, run].rearrange("p (a r f) -> p a r f", a=2, r=RATIO),
+                in0=gate_psum[:].rearrange("p r a f -> p a r f"),
+                in1=ape_f32[:].rearrange("p r a f -> p a r f"),
                 op=ALU.add,
             )
             nc.scalar.copy(
-                out=values[:, j + 1].rearrange("p r h f -> p (r h f)"),
-                in_=kv_psum[:].rearrange("p r c -> p (r c)"),
+                out=values[:, run].rearrange("p (a r f) -> p a r f", a=2, r=RATIO),
+                in_=kv_psum[:].rearrange("p r a f -> p a r f"),
             )
 
-        def hand_down(gates, values):
-            moved = psum_shift.tile([P, 2, RATIO, HD], F32)
-            nc.tensor.matmul(
-                out=moved[:, 0], lhsT=down, rhs=gates[:, WPP, :, NEXT, :], start=True, stop=True
-            )
-            nc.tensor.matmul(
-                out=moved[:, 1], lhsT=down, rhs=values[:, WPP, :, NEXT, :], start=True, stop=True
-            )
+        def move_down(b):
+            moved = psum_sums.tile([P, 2, HALF], F32, tag="flipped")
+            for which in range(2):
+                nc.tensor.matmul(
+                    out=moved[:, which, :], lhsT=down,
+                    rhs=tapes[b][which][:, 2 * WPP * HALF : (2 * WPP + 1) * HALF],
+                    start=True, stop=True,
+                )
+            moved_of[b] = moved
+
+        def take_moved(b):
+            gates, values = tapes[b]
+            moved = moved_of[b]
             nc.vector.tensor_scalar(
-                out=gates[:, 0, :, NEXT, :], in0=moved[:, 0], scalar1=no_window_before[:, 0:1],
+                out=gates[:, 0:HALF], in0=moved[:, 0, :], scalar1=no_window_before[:, 0:1],
                 scalar2=None, op0=ALU.add,
             )
-            nc.scalar.copy(out=values[:, 0, :, NEXT, :], in_=moved[:, 1])
+            nc.scalar.copy(out=values[:, 0:HALF], in_=moved[:, 1, :])
 
-        def pool_windows(b, first, gates, values):
-            last = first + GROUP
-            halves = (
-                (gates[:, first + 1 : last + 1, :, THIS, :], values[:, first + 1 : last + 1, :, THIS, :]),
-                (gates[:, first:last, :, NEXT, :], values[:, first:last, :, NEXT, :]),
-            )
-            top_4 = work.tile([P, GROUP, RATIO, HD], F32)
-            nc.vector.tensor_tensor(out=top_4[:], in0=halves[0][0], in1=halves[1][0], op=ALU.max)
+        def first_column(n):
+            return (n % 2) * GROUP * SLOTS * HD
+
+        def run_of(n):
+            return slice(first_column(n), first_column(n) + GROUP * SLOTS * HD)
+
+        def subtract_top(n):
+            gates = tapes[n // 2][0]
+            g = gates[:, run_of(n)].rearrange("p (w s f) -> p w s f", s=SLOTS, f=HD)
+            top_4 = work.tile([P, GROUP, 4, HD], F32)
+            nc.vector.tensor_tensor(out=top_4[:], in0=g[:, :, 0:4, :], in1=g[:, :, 4:8, :], op=ALU.max)
             top_2 = work.tile([P, GROUP, 2, HD], F32)
             nc.vector.tensor_tensor(
                 out=top_2[:], in0=top_4[:, :, 0:2, :], in1=top_4[:, :, 2:4, :], op=ALU.max
             )
             top = work.tile([P, GROUP, HD], F32)
             nc.vector.tensor_tensor(out=top[:], in0=top_2[:, :, 0, :], in1=top_2[:, :, 1, :], op=ALU.max)
-            for g, v in halves:
-                nc.vector.tensor_tensor(
-                    out=g, in0=g, in1=top[:].unsqueeze(2).to_broadcast([P, GROUP, RATIO, HD]),
-                    op=ALU.subtract,
-                )
-                nc.scalar.activation(out=g, in_=g, func=ACT.Exp)
-            for g, v in halves:
-                nc.vector.tensor_tensor(out=v, in0=v, in1=g, op=ALU.mult)
-            sums_4 = work.tile([P, 2, GROUP, RATIO, HD], F32)
-            for which in range(2):
-                nc.vector.tensor_tensor(
-                    out=sums_4[:, which], in0=halves[0][which], in1=halves[1][which], op=ALU.add
-                )
-            sums_2 = work.tile([P, 2, GROUP, 2, HD], F32)
             nc.vector.tensor_tensor(
-                out=sums_2[:], in0=sums_4[:, :, :, 0:2, :], in1=sums_4[:, :, :, 2:4, :], op=ALU.add
+                out=g, in0=g, in1=top[:].unsqueeze(2).to_broadcast([P, GROUP, SLOTS, HD]),
+                op=ALU.subtract,
             )
-            sums = work.tile([P, 2, GROUP, HD], F32)
+
+        def exponentiate(n):
+            gates = tapes[n // 2][0]
+            nc.scalar.activation(out=gates[:, run_of(n)], in_=gates[:, run_of(n)], func=ACT.Exp)
+
+        def weigh(n):
+            gates, values = tapes[n // 2]
             nc.vector.tensor_tensor(
-                out=sums[:], in0=sums_2[:, :, :, 0, :], in1=sums_2[:, :, :, 1, :], op=ALU.add
+                out=values[:, run_of(n)], in0=values[:, run_of(n)], in1=gates[:, run_of(n)], op=ALU.mult
             )
+
+        def add_slots(n, which):
+            tape = tapes[n // 2][which]
+            flipped = psum_sums.tile([P, GROUP, P], F32)
+            for w in range(GROUP):
+                for two in range(SLOTS // 2):
+                    start = first_column(n) + w * SLOTS * HD + two * P
+                    nc.tensor.matmul(
+                        out=flipped[:, w, :], lhsT=tape[:, start : start + P], rhs=identity[:],
+                        is_transpose=True, start=(two == 0), stop=(two == SLOTS // 2 - 1),
+                    )
+            flipped_sbuf = work.tile([P, GROUP, P], F32)
+            nc.scalar.copy(out=flipped_sbuf[:], in_=flipped[:])
+            flipped_of[(n, which)] = flipped_sbuf
+
+        def add_parities(n, which):
+            if which == 0:
+                sums = psum_sums.tile([P, 2, GROUP, HD], F32)
+                sums_of[n] = sums
+            for w in range(GROUP):
+                nc.tensor.matmul(
+                    out=sums_of[n][:, which, w, :], lhsT=flipped_of[(n, which)][:, w, :],
+                    rhs=both_parities[:], start=True, stop=True,
+                )
+
+        def finish(n):
+            first = (n % 2) * GROUP
+            sums = sums_of[n]
             inverse = work.tile([P, GROUP, HD], F32)
             nc.vector.reciprocal(out=inverse[:], in_=sums[:, 0])
             pooled = work.tile([P, GROUP, HD], F32)
             nc.vector.tensor_tensor(out=pooled[:], in0=sums[:, 1], in1=inverse[:], op=ALU.mult)
-
             products = work.tile([P, GROUP, 2, ROPE], F32)
             nc.vector.tensor_tensor(
                 out=products[:],
                 in0=pooled[:, :, HD - ROPE : HD].unsqueeze(2).to_broadcast([P, GROUP, 2, ROPE]),
-                in1=table[:, first:last].rearrange("p w o j i -> p w o (j i)"),
+                in1=table_of[0][:, first : first + GROUP].rearrange("p w o j i -> p w o (j i)"),
                 op=ALU.mult,
             )
-            rotated = work.tile([P, GROUP, HD], F32)
+            rotated = work.tile([P, GROUP, ROPE], F32)
             nc.vector.tensor_reduce(
-                out=rotated[:, :, HD - ROPE : HD].rearrange("p w (j o) -> p w o j", o=2),
+                out=rotated[:].rearrange("p w (j o) -> p w o j", o=2),
                 in_=products[:].rearrange("p w o (j i) -> p w o j i", i=2),
                 axis=AXIS.X,
                 op=ALU.add,
             )
-            nc.scalar.copy(out=rotated[:, :, 0 : HD - ROPE], in_=pooled[:, :, 0 : HD - ROPE])
-            for out, result in ((out_0, rotated), (out_1, pooled)):
-                nc.sync.dma_start(
-                    out=out[b].rearrange("(p w) f -> p w f", w=WPP)[:, first:last, :], in_=result[:]
-                )
+            k_rot, plain = (
+                out[n // 2].rearrange("(p w) f -> p w f", w=WPP)[:, first : first + GROUP, :]
+                for out in (out_0, out_1)
+            )
+            nc.sync.dma_start(out=plain, in_=pooled[:])
+            nc.sync.dma_start(out=k_rot[:, :, 0 : HD - ROPE], in_=pooled[:, :, 0 : HD - ROPE])
+            nc.sync.dma_start(out=k_rot[:, :, HD - ROPE : HD], in_=rotated[:])
 
-        for b in range(BATCH):
-            gates = sequence.tile([P, WPP + 1, RATIO, 2, HD], F32)
-            values = sequence.tile([P, WPP + 1, RATIO, 2, HD], F32)
-            project(b, WPP - 1, gates, values)
-            hand_down(gates, values)
-            for j in range(WPP - 1):
-                project(b, j, gates, values)
-                if (j + 1) % GROUP == 0:
-                    pool_windows(b, j + 1 - GROUP, gates, values)
-            pool_windows(b, WPP - GROUP, gates, values)
+        def group_due(step):
+            n = step // GROUP - 1
+            return n if step % GROUP == 0 and 0 <= n < GROUPS else None
+
+        with tc.manual_schedule():
+            for g in range(LOADS_AHEAD - FLIPS_AHEAD):
+                load(g)
+            for step in range(-FLIPS_AHEAD, UNITS + GROUP + 1):
+                if step + LOADS_AHEAD < UNITS:
+                    load(step + LOADS_AHEAD)
+                if group_due(step - 4) is not None:
+                    add_parities(group_due(step - 4), 1)
+                if step + FLIPS_AHEAD < UNITS:
+                    flip_words(step + FLIPS_AHEAD)
+                if 0 <= step + 1 < UNITS:
+                    quantise(step + 1)
+                if 0 <= step < UNITS:
+                    land(step)
+                if 0 <= step + 1 < UNITS:
+                    project(step + 1)
+                if step == 0:
+                    table_of[0] = rope_table(nc, const, rest)
+                if 0 <= step - 1 < UNITS and (step - 1) % WPP == 0:
+                    move_down((step - 1) // WPP)
+                if 0 <= step - 2 < UNITS and (step - 2) % WPP == 0:
+                    take_moved((step - 2) // WPP)
+                if group_due(step) is not None:
+                    subtract_top(group_due(step))
+                if group_due(step - 4) is not None:
+                    finish(group_due(step - 4))
+                if group_due(step - 1) is not None:
+                    exponentiate(group_due(step - 1))
+                if group_due(step - 2) is not None:
+                    add_slots(group_due(step - 2), 0)
+                    weigh(group_due(step - 2))
+                if group_due(step - 3) is not None:
+                    add_parities(group_due(step - 3), 0)
+                    add_slots(group_due(step - 3), 1)

@@ -187,6 +187,7 @@ def tile_deepseekv4attention_pa_t_kernel(tc, hidden, wkv, wgate, ape, out_0, out
 
         loaded, grouped_words_of, operand_of, products_of, tapes = {}, {}, {}, {}, {}
         moved_of, flipped_of, sums_of, table_of = {}, {}, {}, {}
+        top_of, inverse_of, pooled_of, products_rope_of = {}, {}, {}, {}
 
         def load(g):
             j = (g - 1) % WPP
@@ -290,19 +291,33 @@ def tile_deepseekv4attention_pa_t_kernel(tc, hidden, wkv, wgate, ape, out_0, out
         def run_of(n):
             return slice(first_column(n), first_column(n) + GROUP * SLOTS * HD)
 
-        def subtract_top(n):
-            gates = tapes[n // 2][0]
-            g = gates[:, run_of(n)].rearrange("p (w s f) -> p w s f", s=SLOTS, f=HD)
+        def slots_of(n):
+            return tapes[n // 2][0][:, run_of(n)].rearrange("p (w s f) -> p w s f", s=SLOTS, f=HD)
+
+        def top_of_4(n):
+            g = slots_of(n)
             top_4 = work.tile([P, GROUP, 4, HD], F32)
             nc.vector.tensor_tensor(out=top_4[:], in0=g[:, :, 0:4, :], in1=g[:, :, 4:8, :], op=ALU.max)
+            top_of[n] = top_4
+
+        def top_of_2(n):
+            top_4 = top_of[n]
             top_2 = work.tile([P, GROUP, 2, HD], F32)
             nc.vector.tensor_tensor(
                 out=top_2[:], in0=top_4[:, :, 0:2, :], in1=top_4[:, :, 2:4, :], op=ALU.max
             )
+            top_of[n] = top_2
+
+        def top_of_1(n):
+            top_2 = top_of[n]
             top = work.tile([P, GROUP, HD], F32)
             nc.vector.tensor_tensor(out=top[:], in0=top_2[:, :, 0, :], in1=top_2[:, :, 1, :], op=ALU.max)
+            top_of[n] = top
+
+        def subtract_top(n):
+            g = slots_of(n)
             nc.vector.tensor_tensor(
-                out=g, in0=g, in1=top[:].unsqueeze(2).to_broadcast([P, GROUP, SLOTS, HD]),
+                out=g, in0=g, in1=top_of[n][:].unsqueeze(2).to_broadcast([P, GROUP, SLOTS, HD]),
                 op=ALU.subtract,
             )
 
@@ -326,8 +341,11 @@ def tile_deepseekv4attention_pa_t_kernel(tc, hidden, wkv, wgate, ape, out_0, out
                         out=flipped[:, w, :], lhsT=tape[:, start : start + P], rhs=identity[:],
                         is_transpose=True, start=(two == 0), stop=(two == SLOTS // 2 - 1),
                     )
+            flipped_of[(n, which)] = flipped
+
+        def fetch_flipped(n, which):
             flipped_sbuf = work.tile([P, GROUP, P], F32)
-            nc.scalar.copy(out=flipped_sbuf[:], in_=flipped[:])
+            nc.scalar.copy(out=flipped_sbuf[:], in_=flipped_of[(n, which)][:])
             flipped_of[(n, which)] = flipped_sbuf
 
         def add_parities(n, which):
@@ -340,34 +358,46 @@ def tile_deepseekv4attention_pa_t_kernel(tc, hidden, wkv, wgate, ape, out_0, out
                     rhs=both_parities[:], start=True, stop=True,
                 )
 
-        def finish(n):
+        def rows_of(out, n):
             first = (n % 2) * GROUP
-            sums = sums_of[n]
+            return out[n // 2].rearrange("(p w) f -> p w f", w=WPP)[:, first : first + GROUP, :]
+
+        def invert(n):
             inverse = work.tile([P, GROUP, HD], F32)
-            nc.vector.reciprocal(out=inverse[:], in_=sums[:, 0])
+            nc.vector.reciprocal(out=inverse[:], in_=sums_of[n][:, 0])
+            inverse_of[n] = inverse
+
+        def divide(n):
             pooled = work.tile([P, GROUP, HD], F32)
-            nc.vector.tensor_tensor(out=pooled[:], in0=sums[:, 1], in1=inverse[:], op=ALU.mult)
+            nc.vector.tensor_tensor(
+                out=pooled[:], in0=sums_of[n][:, 1], in1=inverse_of[n][:], op=ALU.mult
+            )
+            nc.sync.dma_start(out=rows_of(out_1, n), in_=pooled[:])
+            nc.sync.dma_start(
+                out=rows_of(out_0, n)[:, :, 0 : HD - ROPE], in_=pooled[:, :, 0 : HD - ROPE]
+            )
+            pooled_of[n] = pooled
+
+        def rotate_products(n):
+            first = (n % 2) * GROUP
             products = work.tile([P, GROUP, 2, ROPE], F32)
             nc.vector.tensor_tensor(
                 out=products[:],
-                in0=pooled[:, :, HD - ROPE : HD].unsqueeze(2).to_broadcast([P, GROUP, 2, ROPE]),
+                in0=pooled_of[n][:, :, HD - ROPE : HD].unsqueeze(2).to_broadcast([P, GROUP, 2, ROPE]),
                 in1=table_of[0][:, first : first + GROUP].rearrange("p w o j i -> p w o (j i)"),
                 op=ALU.mult,
             )
+            products_rope_of[n] = products
+
+        def rotate_sums(n):
             rotated = work.tile([P, GROUP, ROPE], F32)
             nc.vector.tensor_reduce(
                 out=rotated[:].rearrange("p w (j o) -> p w o j", o=2),
-                in_=products[:].rearrange("p w o (j i) -> p w o j i", i=2),
+                in_=products_rope_of[n][:].rearrange("p w o (j i) -> p w o j i", i=2),
                 axis=AXIS.X,
                 op=ALU.add,
             )
-            k_rot, plain = (
-                out[n // 2].rearrange("(p w) f -> p w f", w=WPP)[:, first : first + GROUP, :]
-                for out in (out_0, out_1)
-            )
-            nc.sync.dma_start(out=plain, in_=pooled[:])
-            nc.sync.dma_start(out=k_rot[:, :, 0 : HD - ROPE], in_=pooled[:, :, 0 : HD - ROPE])
-            nc.sync.dma_start(out=k_rot[:, :, HD - ROPE : HD], in_=rotated[:])
+            nc.sync.dma_start(out=rows_of(out_0, n)[:, :, HD - ROPE : HD], in_=rotated[:])
 
         def group_due(step):
             n = step // GROUP - 1
@@ -376,34 +406,52 @@ def tile_deepseekv4attention_pa_t_kernel(tc, hidden, wkv, wgate, ape, out_0, out
         with tc.manual_schedule():
             for g in range(LOADS_AHEAD - FLIPS_AHEAD):
                 load(g)
-            for step in range(-FLIPS_AHEAD, UNITS + GROUP + 1):
+            for step in range(-FLIPS_AHEAD, UNITS + 2 * GROUP + 1):
+                due = [group_due(step - k) for k in range(2 * GROUP + 1)]
                 if step + LOADS_AHEAD < UNITS:
                     load(step + LOADS_AHEAD)
-                if group_due(step - 4) is not None:
-                    add_parities(group_due(step - 4), 1)
+                if due[2] is not None:
+                    exponentiate(due[2])
+                if due[4] is not None:
+                    fetch_flipped(due[4], 0)
+                if due[5] is not None:
+                    fetch_flipped(due[5], 1)
                 if step + FLIPS_AHEAD < UNITS:
                     flip_words(step + FLIPS_AHEAD)
+                if due[1] is not None:
+                    top_of_1(due[1])
                 if 0 <= step + 1 < UNITS:
                     quantise(step + 1)
+                    project(step + 1)
                 if 0 <= step < UNITS:
                     land(step)
-                if 0 <= step + 1 < UNITS:
-                    project(step + 1)
+                if due[0] is not None:
+                    top_of_4(due[0])
+                if due[7] is not None:
+                    invert(due[7])
+                if due[8] is not None:
+                    rotate_products(due[8])
+                if due[3] is not None:
+                    weigh(due[3])
+                if due[1] is not None:
+                    subtract_top(due[1])
+                if due[0] is not None:
+                    top_of_2(due[0])
+                if due[7] is not None:
+                    divide(due[7])
+                if due[8] is not None:
+                    rotate_sums(due[8])
                 if step == 0:
                     table_of[0] = rope_table(nc, const, rest)
                 if 0 <= step - 1 < UNITS and (step - 1) % WPP == 0:
                     move_down((step - 1) // WPP)
                 if 0 <= step - 2 < UNITS and (step - 2) % WPP == 0:
                     take_moved((step - 2) // WPP)
-                if group_due(step) is not None:
-                    subtract_top(group_due(step))
-                if group_due(step - 4) is not None:
-                    finish(group_due(step - 4))
-                if group_due(step - 1) is not None:
-                    exponentiate(group_due(step - 1))
-                if group_due(step - 2) is not None:
-                    add_slots(group_due(step - 2), 0)
-                    weigh(group_due(step - 2))
-                if group_due(step - 3) is not None:
-                    add_parities(group_due(step - 3), 0)
-                    add_slots(group_due(step - 3), 1)
+                if due[3] is not None:
+                    add_slots(due[3], 0)
+                if due[4] is not None:
+                    add_slots(due[4], 1)
+                if due[5] is not None:
+                    add_parities(due[5], 0)
+                if due[6] is not None:
+                    add_parities(due[6], 1)

@@ -152,7 +152,7 @@ def tile_deepseekv4attention_pa_t_kernel(tc, hidden, wkv, wgate, ape, out_0, out
         words = ctx.enter_context(tc.tile_pool(name="words", bufs=FLIPS_AHEAD + 1))
         operand = ctx.enter_context(tc.tile_pool(name="operand", bufs=2))
         sequence = ctx.enter_context(tc.tile_pool(name="sequence", bufs=2))
-        work = ctx.enter_context(tc.tile_pool(name="work", bufs=2))
+        work = ctx.enter_context(tc.tile_pool(name="work", bufs=3))
         psum_words = ctx.enter_context(tc.psum_pool(name="psum_words", bufs=2))
         psum_proj = ctx.enter_context(tc.psum_pool(name="psum_proj", bufs=2))
         psum_sums = ctx.enter_context(tc.psum_pool(name="psum_sums", bufs=1))
@@ -381,7 +381,7 @@ def tile_deepseekv4attention_pa_t_kernel(tc, hidden, wkv, wgate, ape, out_0, out
         def rotate_products(n):
             first = (n % 2) * GROUP
             products = work.tile([P, GROUP, 2, ROPE], F32)
-            nc.vector.tensor_tensor(
+            nc.gpsimd.tensor_tensor(
                 out=products[:],
                 in0=pooled_of[n][:, :, HD - ROPE : HD].unsqueeze(2).to_broadcast([P, GROUP, 2, ROPE]),
                 in1=table_of[0][:, first : first + GROUP].rearrange("p w o j i -> p w o (j i)"),
@@ -391,10 +391,11 @@ def tile_deepseekv4attention_pa_t_kernel(tc, hidden, wkv, wgate, ape, out_0, out
 
         def rotate_sums(n):
             rotated = work.tile([P, GROUP, ROPE], F32)
-            nc.vector.tensor_reduce(
+            pairs = products_rope_of[n][:].rearrange("p w o (j i) -> p w o j i", i=2)
+            nc.gpsimd.tensor_tensor(
                 out=rotated[:].rearrange("p w (j o) -> p w o j", o=2),
-                in_=products_rope_of[n][:].rearrange("p w o (j i) -> p w o j i", i=2),
-                axis=AXIS.X,
+                in0=pairs[:, :, :, :, 0],
+                in1=pairs[:, :, :, :, 1],
                 op=ALU.add,
             )
             nc.sync.dma_start(out=rows_of(out_0, n)[:, :, HD - ROPE : HD], in_=rotated[:])
@@ -403,55 +404,54 @@ def tile_deepseekv4attention_pa_t_kernel(tc, hidden, wkv, wgate, ape, out_0, out
             n = step // GROUP - 1
             return n if step % GROUP == 0 and 0 <= n < GROUPS else None
 
-        with tc.manual_schedule():
-            for g in range(LOADS_AHEAD - FLIPS_AHEAD):
-                load(g)
-            for step in range(-FLIPS_AHEAD, UNITS + 2 * GROUP + 1):
-                due = [group_due(step - k) for k in range(2 * GROUP + 1)]
-                if step + LOADS_AHEAD < UNITS:
-                    load(step + LOADS_AHEAD)
-                if due[2] is not None:
-                    exponentiate(due[2])
-                if due[4] is not None:
-                    fetch_flipped(due[4], 0)
-                if due[5] is not None:
-                    fetch_flipped(due[5], 1)
-                if step + FLIPS_AHEAD < UNITS:
-                    flip_words(step + FLIPS_AHEAD)
-                if due[1] is not None:
-                    top_of_1(due[1])
-                if 0 <= step + 1 < UNITS:
-                    quantise(step + 1)
-                    project(step + 1)
-                if 0 <= step < UNITS:
-                    land(step)
-                if due[0] is not None:
-                    top_of_4(due[0])
-                if due[7] is not None:
-                    invert(due[7])
-                if due[8] is not None:
-                    rotate_products(due[8])
-                if due[3] is not None:
-                    weigh(due[3])
-                if due[1] is not None:
-                    subtract_top(due[1])
-                if due[0] is not None:
-                    top_of_2(due[0])
-                if due[7] is not None:
-                    divide(due[7])
-                if due[8] is not None:
-                    rotate_sums(due[8])
-                if step == 0:
-                    table_of[0] = rope_table(nc, const, rest)
-                if 0 <= step - 1 < UNITS and (step - 1) % WPP == 0:
-                    move_down((step - 1) // WPP)
-                if 0 <= step - 2 < UNITS and (step - 2) % WPP == 0:
-                    take_moved((step - 2) // WPP)
-                if due[3] is not None:
-                    add_slots(due[3], 0)
-                if due[4] is not None:
-                    add_slots(due[4], 1)
-                if due[5] is not None:
-                    add_parities(due[5], 0)
-                if due[6] is not None:
-                    add_parities(due[6], 1)
+        for g in range(LOADS_AHEAD - FLIPS_AHEAD):
+            load(g)
+        for step in range(-FLIPS_AHEAD, UNITS + 2 * GROUP + 1):
+            due = [group_due(step - k) for k in range(2 * GROUP + 1)]
+            if step + LOADS_AHEAD < UNITS:
+                load(step + LOADS_AHEAD)
+            if due[2] is not None:
+                exponentiate(due[2])
+            if due[4] is not None:
+                fetch_flipped(due[4], 0)
+            if due[5] is not None:
+                fetch_flipped(due[5], 1)
+            if step + FLIPS_AHEAD < UNITS:
+                flip_words(step + FLIPS_AHEAD)
+            if due[1] is not None:
+                top_of_1(due[1])
+            if 0 <= step + 1 < UNITS:
+                quantise(step + 1)
+                project(step + 1)
+            if 0 <= step < UNITS:
+                land(step)
+            if due[0] is not None:
+                top_of_4(due[0])
+            if due[7] is not None:
+                invert(due[7])
+            if due[8] is not None:
+                rotate_products(due[8])
+            if due[3] is not None:
+                weigh(due[3])
+            if due[1] is not None:
+                subtract_top(due[1])
+            if due[0] is not None:
+                top_of_2(due[0])
+            if due[7] is not None:
+                divide(due[7])
+            if due[8] is not None:
+                rotate_sums(due[8])
+            if step == 0:
+                table_of[0] = rope_table(nc, const, rest)
+            if 0 <= step - 1 < UNITS and (step - 1) % WPP == 0:
+                move_down((step - 1) // WPP)
+            if 0 <= step - 2 < UNITS and (step - 2) % WPP == 0:
+                take_moved((step - 2) // WPP)
+            if due[3] is not None:
+                add_slots(due[3], 0)
+            if due[4] is not None:
+                add_slots(due[4], 1)
+            if due[5] is not None:
+                add_parities(due[5], 0)
+            if due[6] is not None:
+                add_parities(due[6], 1)

@@ -12,7 +12,6 @@ U8 = mybir.dt.uint8
 FP8X4 = mybir.dt.float8_e4m3fn_x4
 ALU = mybir.AluOpType
 ACT = mybir.ActivationFunctionType
-AXIS = mybir.AxisListType
 
 P = 128
 BATCH, SEQ, HID = 4, 4096, 512
@@ -26,11 +25,11 @@ WPP = SEQ // RATIO // P
 WORDS = HID // 2
 GROUP = 4
 UNITS = BATCH * WPP
-GROUPS = UNITS // GROUP
 LOADS_AHEAD = 7
 FLIPS_AHEAD = 3
 SLOTS = 2 * RATIO
-HALF = RATIO * HD
+ENTRIES = WPP + 1
+ROW = ENTRIES * HD
 MINUS_BIG = -1.0e30
 ROUND_MAGIC = 1.5 * 2.0**23
 
@@ -157,6 +156,20 @@ def tile_deepseekv4attention_pa_t_kernel(tc, hidden, wkv, wgate, ape, out_0, out
         psum_proj = ctx.enter_context(tc.psum_pool(name="psum_proj", bufs=2))
         psum_sums = ctx.enter_context(tc.psum_pool(name="psum_sums", bufs=1))
 
+        loaded = {}
+
+        def load(g):
+            j = (g - 1) % WPP
+            x = tokens.tile([P, RATIO * HID], BF16)
+            nc.sync.dma_start(
+                out=x[:],
+                in_=hidden[g // WPP].rearrange("(p t) k -> p (t k)", t=RATIO * WPP)[
+                    :, j * RATIO * HID : (j + 1) * RATIO * HID
+                ],
+            )
+            loaded[g] = x
+
+        load(0)
         rest = rope_angles(nc, const)
         w_codes, w_scales = quantise_weights(nc, const, wgate, wkv)
 
@@ -171,10 +184,6 @@ def tile_deepseekv4attention_pa_t_kernel(tc, hidden, wkv, wgate, ape, out_0, out
 
         identity = const.tile([P, P], F32)
         make_identity(nc, identity[:])
-        both_parities = const.tile([P, HD], F32)
-        nc.vector.tensor_tensor(
-            out=both_parities[:], in0=identity[:, 0:HD], in1=identity[:, HD:P], op=ALU.add
-        )
         padded = const.tile([P, P + 1], F32)
         nc.gpsimd.memset(padded[:, 0:1], 0.0)
         make_identity(nc, padded[:, 1 : P + 1])
@@ -185,20 +194,17 @@ def tile_deepseekv4attention_pa_t_kernel(tc, hidden, wkv, wgate, ape, out_0, out
             op0=ALU.mult,
         )
 
-        loaded, grouped_words_of, operand_of, products_of, tapes = {}, {}, {}, {}, {}
+        def by_slot(tape):
+            return tape[:, 0 : SLOTS * ROW].rearrange("p (s i f) -> p s i f", s=SLOTS, i=ENTRIES)
+
+        def unit_view(tape, j):
+            apart = RATIO * ROW + HD
+            both = tape[:, j * HD : j * HD + 2 * apart].rearrange("p (a x) -> p a x", a=2)
+            return both[:, :, 0 : RATIO * ROW].rearrange("p a (r y) -> p a r y", y=ROW)[:, :, :, 0:HD]
+
+        grouped_words_of, operand_of, products_of, tapes = {}, {}, {}, {}
         moved_of, flipped_of, sums_of, table_of = {}, {}, {}, {}
         top_of, inverse_of, pooled_of, products_rope_of = {}, {}, {}, {}
-
-        def load(g):
-            j = (g - 1) % WPP
-            x = tokens.tile([P, RATIO * HID], BF16)
-            nc.sync.dma_start(
-                out=x[:],
-                in_=hidden[g // WPP].rearrange("(p t) k -> p (t k)", t=RATIO * WPP)[
-                    :, j * RATIO * HID : (j + 1) * RATIO * HID
-                ],
-            )
-            loaded[g] = x
 
         def flip_words(g):
             x_words = loaded[g][:].bitcast(F32)
@@ -248,30 +254,28 @@ def tile_deepseekv4attention_pa_t_kernel(tc, hidden, wkv, wgate, ape, out_0, out
 
         def land(g):
             if g % WPP == 0:
-                gates = sequence.tile([P, (2 * WPP + 1) * HALF], F32)
-                values = sequence.tile([P, (2 * WPP + 1) * HALF], F32)
+                gates = sequence.tile([P, (SLOTS + 1) * ROW], F32)
+                values = sequence.tile([P, (SLOTS + 1) * ROW], F32)
                 tapes[g // WPP] = (gates, values)
             gates, values = tapes[g // WPP]
             gate_psum, kv_psum = products_of[g]
             j = (g - 1) % WPP
-            run = slice(HALF + j * 2 * HALF, HALF + (j + 1) * 2 * HALF)
             nc.vector.tensor_tensor(
-                out=gates[:, run].rearrange("p (a r f) -> p a r f", a=2, r=RATIO),
+                out=unit_view(gates, j),
                 in0=gate_psum[:].rearrange("p r a f -> p a r f"),
                 in1=ape_f32[:].rearrange("p r a f -> p a r f"),
                 op=ALU.add,
             )
             nc.scalar.copy(
-                out=values[:, run].rearrange("p (a r f) -> p a r f", a=2, r=RATIO),
+                out=unit_view(values, j),
                 in_=kv_psum[:].rearrange("p r a f -> p a r f"),
             )
 
         def move_down(b):
-            moved = psum_sums.tile([P, 2, HALF], F32, tag="flipped")
+            moved = psum_sums.tile([P, 2, RATIO, HD], F32, tag="flipped")
             for which in range(2):
                 nc.tensor.matmul(
-                    out=moved[:, which, :], lhsT=down,
-                    rhs=tapes[b][which][:, 2 * WPP * HALF : (2 * WPP + 1) * HALF],
+                    out=moved[:, which], lhsT=down, rhs=by_slot(tapes[b][which])[:, RATIO:SLOTS, WPP, :],
                     start=True, stop=True,
                 )
             moved_of[b] = moved
@@ -280,95 +284,93 @@ def tile_deepseekv4attention_pa_t_kernel(tc, hidden, wkv, wgate, ape, out_0, out
             gates, values = tapes[b]
             moved = moved_of[b]
             nc.vector.tensor_scalar(
-                out=gates[:, 0:HALF], in0=moved[:, 0, :], scalar1=no_window_before[:, 0:1],
+                out=by_slot(gates)[:, RATIO:SLOTS, 0, :], in0=moved[:, 0], scalar1=no_window_before[:, 0:1],
                 scalar2=None, op0=ALU.add,
             )
-            nc.scalar.copy(out=values[:, 0:HALF], in_=moved[:, 1, :])
+            nc.scalar.copy(out=by_slot(values)[:, RATIO:SLOTS, 0, :], in_=moved[:, 1])
 
-        def first_column(n):
-            return (n % 2) * GROUP * SLOTS * HD
+        groups = []
+        for b in range(BATCH):
+            sizes = [GROUP, GROUP] if b < BATCH - 1 else [GROUP, GROUP // 2, GROUP // 2]
+            for i, size in enumerate(sizes):
+                groups.append((b, sum(sizes[:i]), size))
 
-        def run_of(n):
-            return slice(first_column(n), first_column(n) + GROUP * SLOTS * HD)
-
-        def slots_of(n):
-            return tapes[n // 2][0][:, run_of(n)].rearrange("p (w s f) -> p w s f", s=SLOTS, f=HD)
+        def slots_of(n, which):
+            b, first, size = groups[n]
+            return by_slot(tapes[b][which])[:, :, first : first + size, :]
 
         def top_of_4(n):
-            g = slots_of(n)
-            top_4 = work.tile([P, GROUP, 4, HD], F32)
-            nc.vector.tensor_tensor(out=top_4[:], in0=g[:, :, 0:4, :], in1=g[:, :, 4:8, :], op=ALU.max)
+            g = slots_of(n, 0)
+            top_4 = work.tile([P, 4, groups[n][2], HD], F32)
+            nc.vector.tensor_tensor(out=top_4[:], in0=g[:, 0:4], in1=g[:, 4:8], op=ALU.max)
             top_of[n] = top_4
 
         def top_of_2(n):
             top_4 = top_of[n]
-            top_2 = work.tile([P, GROUP, 2, HD], F32)
-            nc.vector.tensor_tensor(
-                out=top_2[:], in0=top_4[:, :, 0:2, :], in1=top_4[:, :, 2:4, :], op=ALU.max
-            )
+            top_2 = work.tile([P, 2, groups[n][2], HD], F32)
+            nc.vector.tensor_tensor(out=top_2[:], in0=top_4[:, 0:2], in1=top_4[:, 2:4], op=ALU.max)
             top_of[n] = top_2
 
         def top_of_1(n):
             top_2 = top_of[n]
-            top = work.tile([P, GROUP, HD], F32)
-            nc.vector.tensor_tensor(out=top[:], in0=top_2[:, :, 0, :], in1=top_2[:, :, 1, :], op=ALU.max)
+            top = work.tile([P, groups[n][2], HD], F32)
+            nc.vector.tensor_tensor(out=top[:], in0=top_2[:, 0], in1=top_2[:, 1], op=ALU.max)
             top_of[n] = top
 
         def subtract_top(n):
-            g = slots_of(n)
+            g = slots_of(n, 0)
             nc.vector.tensor_tensor(
-                out=g, in0=g, in1=top_of[n][:].unsqueeze(2).to_broadcast([P, GROUP, SLOTS, HD]),
+                out=g, in0=g, in1=top_of[n][:].unsqueeze(1).to_broadcast([P, SLOTS, groups[n][2], HD]),
                 op=ALU.subtract,
             )
 
         def exponentiate(n):
-            gates = tapes[n // 2][0]
-            nc.scalar.activation(out=gates[:, run_of(n)], in_=gates[:, run_of(n)], func=ACT.Exp)
+            nc.scalar.activation(out=slots_of(n, 0), in_=slots_of(n, 0), func=ACT.Exp)
 
         def weigh(n):
-            gates, values = tapes[n // 2]
             nc.vector.tensor_tensor(
-                out=values[:, run_of(n)], in0=values[:, run_of(n)], in1=gates[:, run_of(n)], op=ALU.mult
+                out=slots_of(n, 1), in0=slots_of(n, 1), in1=slots_of(n, 0), op=ALU.mult
             )
 
         def add_slots(n, which):
-            tape = tapes[n // 2][which]
-            flipped = psum_sums.tile([P, GROUP, P], F32)
-            for w in range(GROUP):
-                for two in range(SLOTS // 2):
-                    start = first_column(n) + w * SLOTS * HD + two * P
+            flipped = psum_sums.tile([P, groups[n][2] // 2, P], F32)
+            for two in range(groups[n][2] // 2):
+                for s in range(SLOTS):
                     nc.tensor.matmul(
-                        out=flipped[:, w, :], lhsT=tape[:, start : start + P], rhs=identity[:],
-                        is_transpose=True, start=(two == 0), stop=(two == SLOTS // 2 - 1),
+                        out=flipped[:, two, :],
+                        lhsT=slots_of(n, which)[:, s, 2 * two : 2 * two + 2, :].rearrange("p w f -> p (w f)"),
+                        rhs=identity[:],
+                        is_transpose=True, start=(s == 0), stop=(s == SLOTS - 1),
                     )
             flipped_of[(n, which)] = flipped
 
         def fetch_flipped(n, which):
-            flipped_sbuf = work.tile([P, GROUP, P], F32)
+            flipped_sbuf = work.tile([P, groups[n][2] // 2, P], F32)
             nc.scalar.copy(out=flipped_sbuf[:], in_=flipped_of[(n, which)][:])
             flipped_of[(n, which)] = flipped_sbuf
 
-        def add_parities(n, which):
+        def turn_back(n, which):
             if which == 0:
-                sums = psum_sums.tile([P, 2, GROUP, HD], F32)
+                sums = psum_sums.tile([P, 2, groups[n][2], HD], F32)
                 sums_of[n] = sums
-            for w in range(GROUP):
-                nc.tensor.matmul(
-                    out=sums_of[n][:, which, w, :], lhsT=flipped_of[(n, which)][:, w, :],
-                    rhs=both_parities[:], start=True, stop=True,
+            for two in range(groups[n][2] // 2):
+                nc.tensor.transpose(
+                    sums_of[n][:, which, 2 * two : 2 * two + 2, :].rearrange("p w f -> p (w f)"),
+                    flipped_of[(n, which)][:, two, :],
+                    identity[:],
                 )
 
         def rows_of(out, n):
-            first = (n % 2) * GROUP
-            return out[n // 2].rearrange("(p w) f -> p w f", w=WPP)[:, first : first + GROUP, :]
+            b, first, size = groups[n]
+            return out[b].rearrange("(p w) f -> p w f", w=WPP)[:, first : first + size, :]
 
         def invert(n):
-            inverse = work.tile([P, GROUP, HD], F32)
+            inverse = work.tile([P, groups[n][2], HD], F32)
             nc.vector.reciprocal(out=inverse[:], in_=sums_of[n][:, 0])
             inverse_of[n] = inverse
 
         def divide(n):
-            pooled = work.tile([P, GROUP, HD], F32)
+            pooled = work.tile([P, groups[n][2], HD], F32)
             nc.vector.tensor_tensor(
                 out=pooled[:], in0=sums_of[n][:, 1], in1=inverse_of[n][:], op=ALU.mult
             )
@@ -379,18 +381,18 @@ def tile_deepseekv4attention_pa_t_kernel(tc, hidden, wkv, wgate, ape, out_0, out
             pooled_of[n] = pooled
 
         def rotate_products(n):
-            first = (n % 2) * GROUP
-            products = work.tile([P, GROUP, 2, ROPE], F32)
+            b, first, size = groups[n]
+            products = work.tile([P, size, 2, ROPE], F32)
             nc.gpsimd.tensor_tensor(
                 out=products[:],
-                in0=pooled_of[n][:, :, HD - ROPE : HD].unsqueeze(2).to_broadcast([P, GROUP, 2, ROPE]),
-                in1=table_of[0][:, first : first + GROUP].rearrange("p w o j i -> p w o (j i)"),
+                in0=pooled_of[n][:, :, HD - ROPE : HD].unsqueeze(2).to_broadcast([P, size, 2, ROPE]),
+                in1=table_of[0][:, first : first + size].rearrange("p w o j i -> p w o (j i)"),
                 op=ALU.mult,
             )
             products_rope_of[n] = products
 
         def rotate_sums(n):
-            rotated = work.tile([P, GROUP, ROPE], F32)
+            rotated = work.tile([P, groups[n][2], ROPE], F32)
             pairs = products_rope_of[n][:].rearrange("p w o (j i) -> p w o j i", i=2)
             nc.gpsimd.tensor_tensor(
                 out=rotated[:].rearrange("p w (j o) -> p w o j", o=2),
@@ -401,10 +403,12 @@ def tile_deepseekv4attention_pa_t_kernel(tc, hidden, wkv, wgate, ape, out_0, out
             nc.sync.dma_start(out=rows_of(out_0, n)[:, :, HD - ROPE : HD], in_=rotated[:])
 
         def group_due(step):
-            n = step // GROUP - 1
-            return n if step % GROUP == 0 and 0 <= n < GROUPS else None
+            for n, (b, first, size) in enumerate(groups):
+                if step == b * WPP + first + size:
+                    return n
+            return None
 
-        for g in range(LOADS_AHEAD - FLIPS_AHEAD):
+        for g in range(1, LOADS_AHEAD - FLIPS_AHEAD):
             load(g)
         for step in range(-FLIPS_AHEAD, UNITS + 2 * GROUP + 1):
             due = [group_due(step - k) for k in range(2 * GROUP + 1)]
@@ -452,6 +456,6 @@ def tile_deepseekv4attention_pa_t_kernel(tc, hidden, wkv, wgate, ape, out_0, out
             if due[4] is not None:
                 add_slots(due[4], 1)
             if due[5] is not None:
-                add_parities(due[5], 0)
+                turn_back(due[5], 0)
             if due[6] is not None:
-                add_parities(due[6], 1)
+                turn_back(due[6], 1)

from contextlib import ExitStack
import math

import concourse.mybir as mybir
from concourse.masks import make_identity

F32 = mybir.dt.float32
BF16 = mybir.dt.bfloat16
I32 = mybir.dt.int32
U32 = mybir.dt.uint32
U8 = mybir.dt.uint8
FP8X4 = mybir.dt.float8_e4m3fn_x4
ALU = mybir.AluOpType
ACT = mybir.ActivationFunctionType

P = 128
BATCH, SEQ, HID = 4, 4096, 512
RATIO = 4
HD = 64
FEAT = 2 * HD
ROPE = 32
PAIRS = ROPE // 2
THETA = 10000.0
WPP = SEQ // RATIO // P
WORDS = HID // 2
GROUP = 4
UNITS = BATCH * WPP
LOADS_AHEAD = 7
FLIPS_AHEAD = 3
SLOTS = 2 * RATIO
ENTRIES = WPP + 1
ROW = ENTRIES * HD
MINUS_BIG = -1.0e30
ROUND_MAGIC = 1.5 * 2.0**23

FLOPS = 2 * BATCH * SEQ * HID * 2 * FEAT


def leading_bits(x, bits):
    if x == 0.0:
        return 0.0
    step = 1.0
    while abs(x) / step >= 2.0**bits:
        step *= 2.0
    while abs(x) / step < 2.0 ** (bits - 1):
        step /= 2.0
    return round(x / step) * step


def quantise_weights(nc, const, wgate, wkv):
    raw = const.tile([P, 4, 2, FEAT], BF16)
    for m, w in enumerate((wgate, wkv)):
        for u in range(2):
            nc.sync.dma_start(
                out=raw[:, 2 * u : 2 * u + 2, m, :],
                in_=w[WORDS * u : WORDS * (u + 1), :].rearrange("(q e) c -> q e c", e=2),
            )
    grouped = const.tile([P, 2, 2, HD, 4], BF16, align_bytes=64)
    for a in range(2):
        nc.vector.tensor_copy(
            out=grouped[:, :, 1 - a, :, :],
            in_=raw[:, :, :, a * HD : (a + 1) * HD].rearrange("q t m f -> q m f t"),
        )
    w_codes = const.tile([P, 2 * FEAT], U32, align_bytes=64)
    w_scales = const.tile([P, 2 * FEAT], U8, align_bytes=64)
    nc.vector.quantize_mx(
        out=w_codes[:].bitcast(FP8X4),
        scales=w_scales[:],
        in_=grouped[:].rearrange("q m a f t -> q (m a f t)"),
    )
    return w_codes, w_scales


def rope_angles(nc, const):
    position_int = const.tile([P, WPP], I32)
    nc.gpsimd.iota(position_int[:], pattern=[[RATIO, WPP]], base=0, channel_multiplier=RATIO * WPP)
    position = const.tile([P, WPP], F32)
    nc.vector.tensor_copy(out=position[:], in_=position_int[:])

    angle_hi = const.tile([P, WPP, PAIRS], F32)
    angle_lo = const.tile([P, WPP, PAIRS], F32)
    for j in range(PAIRS):
        frequency = 1.0 / THETA ** (j / PAIRS)
        leading = leading_bits(frequency, 12)
        for angle, factor in ((angle_hi, leading), (angle_lo, frequency - leading)):
            nc.vector.tensor_scalar(
                out=angle[:, :, j], in0=position[:], scalar1=factor, scalar2=None, op0=ALU.mult
            )

    turns = const.tile([P, WPP, PAIRS], F32)
    nc.vector.tensor_tensor(out=turns[:], in0=angle_hi[:], in1=angle_lo[:], op=ALU.add)
    nc.vector.tensor_scalar(
        out=turns[:], in0=turns[:], scalar1=1.0 / (2.0 * math.pi), scalar2=ROUND_MAGIC,
        op0=ALU.mult, op1=ALU.add,
    )
    nc.vector.tensor_scalar(
        out=turns[:], in0=turns[:], scalar1=ROUND_MAGIC, scalar2=None, op0=ALU.subtract
    )

    piece_1 = leading_bits(2.0 * math.pi, 12)
    piece_2 = leading_bits(2.0 * math.pi - piece_1, 12)
    piece_3 = 2.0 * math.pi - piece_1 - piece_2
    rest = const.tile([P, WPP, PAIRS], F32)
    nc.vector.scalar_tensor_tensor(
        out=rest[:], in0=turns[:], scalar=-piece_1, in1=angle_hi[:], op0=ALU.mult, op1=ALU.add
    )
    nc.vector.scalar_tensor_tensor(
        out=rest[:], in0=turns[:], scalar=-piece_2, in1=rest[:], op0=ALU.mult, op1=ALU.add
    )
    nc.vector.tensor_tensor(out=rest[:], in0=rest[:], in1=angle_lo[:], op=ALU.add)
    nc.vector.scalar_tensor_tensor(
        out=rest[:], in0=turns[:], scalar=-piece_3, in1=rest[:], op0=ALU.mult, op1=ALU.add
    )
    return rest


def rope_table(nc, const, rest):
    sin_half = const.tile([P, WPP, PAIRS], F32)
    sin_quarter = const.tile([P, WPP, PAIRS], F32)
    nc.scalar.activation(out=sin_half[:], in_=rest[:], func=ACT.Sin, scale=0.5)
    nc.scalar.activation(out=sin_quarter[:], in_=rest[:], func=ACT.Sin, scale=0.25)
    cos_half = const.tile([P, WPP, PAIRS], F32)
    nc.gpsimd.tensor_tensor(out=cos_half[:], in0=sin_quarter[:], in1=sin_quarter[:], op=ALU.mult)
    nc.gpsimd.tensor_scalar(
        out=cos_half[:], in0=cos_half[:], scalar1=-2.0, scalar2=1.0, op0=ALU.mult, op1=ALU.add
    )
    half_of_sin = const.tile([P, WPP, PAIRS], F32)
    nc.gpsimd.tensor_tensor(out=half_of_sin[:], in0=sin_half[:], in1=cos_half[:], op=ALU.mult)
    square = const.tile([P, WPP, PAIRS], F32)
    nc.gpsimd.tensor_tensor(out=square[:], in0=sin_half[:], in1=sin_half[:], op=ALU.mult)

    table = const.tile([P, WPP, 2, PAIRS, 2], F32)
    for row, column in ((0, 0), (1, 1)):
        nc.gpsimd.tensor_scalar(
            out=table[:, :, row, :, column], in0=square[:], scalar1=-2.0, scalar2=1.0,
            op0=ALU.mult, op1=ALU.add,
        )
    for row, column, sign in ((0, 1, -2.0), (1, 0, 2.0)):
        nc.gpsimd.tensor_scalar(
            out=table[:, :, row, :, column], in0=half_of_sin[:], scalar1=sign, scalar2=0.0,
            op0=ALU.mult, op1=ALU.add,
        )
    return table


def tile_deepseekv4attention_pa_t_kernel(tc, hidden, wkv, wgate, ape, out_0, out_1):
    nc = tc.nc
    with ExitStack() as ctx:
        const = ctx.enter_context(tc.tile_pool(name="const", bufs=1))
        tokens = ctx.enter_context(tc.tile_pool(name="tokens", bufs=LOADS_AHEAD - FLIPS_AHEAD + 1))
        words = ctx.enter_context(tc.tile_pool(name="words", bufs=FLIPS_AHEAD + 1))
        operand = ctx.enter_context(tc.tile_pool(name="operand", bufs=2))
        sequence = ctx.enter_context(tc.tile_pool(name="sequence", bufs=2))
        work = ctx.enter_context(tc.tile_pool(name="work", bufs=3))
        psum_words = ctx.enter_context(tc.psum_pool(name="psum_words", bufs=2))
        psum_proj = ctx.enter_context(tc.psum_pool(name="psum_proj", bufs=2))
        psum_sums = ctx.enter_context(tc.psum_pool(name="psum_sums", bufs=1))

        loaded = {}

        def load(g):
            j = (g - 1) % WPP
            x = tokens.tile([P, RATIO * HID], BF16)
            nc.sync.dma_start(
                out=x[:],
                in_=hidden[g // WPP].rearrange("(p t) k -> p (t k)", t=RATIO * WPP)[
                    :, j * RATIO * HID : (j + 1) * RATIO * HID
                ],
            )
            loaded[g] = x

        load(0)
        rest = rope_angles(nc, const)
        w_codes, w_scales = quantise_weights(nc, const, wgate, wkv)

        ape_bf16 = const.tile([P, RATIO, FEAT], BF16)
        nc.sync.dma_start(
            out=ape_bf16[:].rearrange("p r c -> p (r c)"),
            in_=ape.rearrange("r c -> (r c)").partition_broadcast(P),
        )
        ape_f32 = const.tile([P, RATIO, 2, HD], F32)
        for a in range(2):
            nc.vector.tensor_copy(out=ape_f32[:, :, 1 - a, :], in_=ape_bf16[:, :, a * HD : (a + 1) * HD])

        identity = const.tile([P, P], F32)
        make_identity(nc, identity[:])
        padded = const.tile([P, P + 1], F32)
        nc.gpsimd.memset(padded[:, 0:1], 0.0)
        make_identity(nc, padded[:, 1 : P + 1])
        down = padded[:, 0:P]
        no_window_before = const.tile([P, 1], F32)
        nc.vector.tensor_scalar(
            out=no_window_before[:], in0=identity[:, 0:1], scalar1=MINUS_BIG, scalar2=None,
            op0=ALU.mult,
        )

        def by_slot(tape):
            return tape[:, 0 : SLOTS * ROW].rearrange("p (s i f) -> p s i f", s=SLOTS, i=ENTRIES)

        def unit_view(tape, j):
            apart = RATIO * ROW + HD
            both = tape[:, j * HD : j * HD + 2 * apart].rearrange("p (a x) -> p a x", a=2)
            return both[:, :, 0 : RATIO * ROW].rearrange("p a (r y) -> p a r y", y=ROW)[:, :, :, 0:HD]

        grouped_words_of, operand_of, products_of, tapes = {}, {}, {}, {}
        moved_of, flipped_of, sums_of, table_of = {}, {}, {}, {}
        top_of, inverse_of, pooled_of, products_rope_of = {}, {}, {}, {}

        def flip_words(g):
            x_words = loaded[g][:].bitcast(F32)
            grouped = words.tile([P, RATIO * P, 4], BF16, align_bytes=64)
            grouped_words = grouped[:].bitcast(F32)
            for pair in range(RATIO // 2):
                planes = psum_words.tile([P, 2, 2 * P], F32)
                for r in (2 * pair, 2 * pair + 1):
                    for u in range(2):
                        nc.tensor.transpose(
                            planes[:, u, (r % 2) * P : (r % 2 + 1) * P],
                            x_words[:, r * WORDS + u * P : r * WORDS + (u + 1) * P],
                            identity[:],
                        )
                nc.scalar.copy(
                    out=grouped_words[:, 2 * pair * P : 2 * (pair + 1) * P, :],
                    in_=planes[:].rearrange("q u c -> q c u"),
                )
            grouped_words_of[g] = grouped

        def quantise(g):
            codes = operand.tile([P, RATIO * P], U32, align_bytes=64)
            scales = operand.tile([P, RATIO * P], U8, align_bytes=64)
            nc.vector.quantize_mx(
                out=codes[:].bitcast(FP8X4),
                scales=scales[:],
                in_=grouped_words_of[g][:].rearrange("q c t -> q (c t)"),
            )
            operand_of[g] = (codes, scales)

        def project(g):
            codes, scales = operand_of[g]
            gate_psum = psum_proj.tile([P, RATIO, 2, HD], F32)
            kv_psum = psum_proj.tile([P, RATIO, 2, HD], F32)
            for r in range(RATIO):
                for psum, first in ((gate_psum, 0), (kv_psum, FEAT)):
                    nc.tensor.matmul_mx(
                        out=psum[:, r].rearrange("p a f -> p (a f)"),
                        lhsT=codes[:, r * P : (r + 1) * P].bitcast(FP8X4),
                        lhsT_scale=scales[:, r * P : (r + 1) * P],
                        rhs=w_codes[:, first : first + FEAT].bitcast(FP8X4),
                        rhs_scale=w_scales[:, first : first + FEAT],
                        start=True,
                        stop=True,
                    )
            products_of[g] = (gate_psum, kv_psum)

        def land(g):
            if g % WPP == 0:
                gates = sequence.tile([P, (SLOTS + 1) * ROW], F32)
                values = sequence.tile([P, (SLOTS + 1) * ROW], F32)
                tapes[g // WPP] = (gates, values)
            gates, values = tapes[g // WPP]
            gate_psum, kv_psum = products_of[g]
            j = (g - 1) % WPP
            nc.vector.tensor_tensor(
                out=unit_view(gates, j),
                in0=gate_psum[:].rearrange("p r a f -> p a r f"),
                in1=ape_f32[:].rearrange("p r a f -> p a r f"),
                op=ALU.add,
            )
            nc.scalar.copy(
                out=unit_view(values, j),
                in_=kv_psum[:].rearrange("p r a f -> p a r f"),
            )

        def move_down(b):
            moved = psum_sums.tile([P, 2, RATIO, HD], F32, tag="flipped")
            for which in range(2):
                nc.tensor.matmul(
                    out=moved[:, which], lhsT=down, rhs=by_slot(tapes[b][which])[:, RATIO:SLOTS, WPP, :],
                    start=True, stop=True,
                )
            moved_of[b] = moved

        def take_moved(b):
            gates, values = tapes[b]
            moved = moved_of[b]
            nc.vector.tensor_scalar(
                out=by_slot(gates)[:, RATIO:SLOTS, 0, :], in0=moved[:, 0], scalar1=no_window_before[:, 0:1],
                scalar2=None, op0=ALU.add,
            )
            nc.scalar.copy(out=by_slot(values)[:, RATIO:SLOTS, 0, :], in_=moved[:, 1])

        groups = []
        for b in range(BATCH):
            sizes = [GROUP, GROUP] if b < BATCH - 1 else [GROUP, GROUP // 2, GROUP // 2]
            for i, size in enumerate(sizes):
                groups.append((b, sum(sizes[:i]), size))

        def slots_of(n, which):
            b, first, size = groups[n]
            return by_slot(tapes[b][which])[:, :, first : first + size, :]

        def top_of_4(n):
            g = slots_of(n, 0)
            top_4 = work.tile([P, 4, groups[n][2], HD], F32)
            nc.vector.tensor_tensor(out=top_4[:], in0=g[:, 0:4], in1=g[:, 4:8], op=ALU.max)
            top_of[n] = top_4

        def top_of_2(n):
            top_4 = top_of[n]
            top_2 = work.tile([P, 2, groups[n][2], HD], F32)
            nc.vector.tensor_tensor(out=top_2[:], in0=top_4[:, 0:2], in1=top_4[:, 2:4], op=ALU.max)
            top_of[n] = top_2

        def top_of_1(n):
            top_2 = top_of[n]
            top = work.tile([P, groups[n][2], HD], F32)
            nc.vector.tensor_tensor(out=top[:], in0=top_2[:, 0], in1=top_2[:, 1], op=ALU.max)
            top_of[n] = top

        def subtract_top(n):
            g = slots_of(n, 0)
            nc.vector.tensor_tensor(
                out=g, in0=g, in1=top_of[n][:].unsqueeze(1).to_broadcast([P, SLOTS, groups[n][2], HD]),
                op=ALU.subtract,
            )

        def exponentiate(n):
            nc.scalar.activation(out=slots_of(n, 0), in_=slots_of(n, 0), func=ACT.Exp)

        def weigh(n):
            nc.vector.tensor_tensor(
                out=slots_of(n, 1), in0=slots_of(n, 1), in1=slots_of(n, 0), op=ALU.mult
            )

        def add_slots(n, which):
            flipped = psum_sums.tile([P, groups[n][2] // 2, P], F32)
            for two in range(groups[n][2] // 2):
                for s in range(SLOTS):
                    nc.tensor.matmul(
                        out=flipped[:, two, :],
                        lhsT=slots_of(n, which)[:, s, 2 * two : 2 * two + 2, :].rearrange("p w f -> p (w f)"),
                        rhs=identity[:],
                        is_transpose=True, start=(s == 0), stop=(s == SLOTS - 1),
                    )
            flipped_of[(n, which)] = flipped

        def fetch_flipped(n, which):
            flipped_sbuf = work.tile([P, groups[n][2] // 2, P], F32)
            nc.scalar.copy(out=flipped_sbuf[:], in_=flipped_of[(n, which)][:])
            flipped_of[(n, which)] = flipped_sbuf

        def turn_back(n, which):
            if which == 0:
                sums = psum_sums.tile([P, 2, groups[n][2], HD], F32)
                sums_of[n] = sums
            for two in range(groups[n][2] // 2):
                nc.tensor.transpose(
                    sums_of[n][:, which, 2 * two : 2 * two + 2, :].rearrange("p w f -> p (w f)"),
                    flipped_of[(n, which)][:, two, :],
                    identity[:],
                )

        def rows_of(out, n):
            b, first, size = groups[n]
            return out[b].rearrange("(p w) f -> p w f", w=WPP)[:, first : first + size, :]

        def invert(n):
            inverse = work.tile([P, groups[n][2], HD], F32)
            nc.vector.reciprocal(out=inverse[:], in_=sums_of[n][:, 0])
            inverse_of[n] = inverse

        def divide(n):
            pooled = work.tile([P, groups[n][2], HD], F32)
            nc.vector.tensor_tensor(
                out=pooled[:], in0=sums_of[n][:, 1], in1=inverse_of[n][:], op=ALU.mult
            )
            nc.sync.dma_start(out=rows_of(out_1, n), in_=pooled[:])
            nc.sync.dma_start(
                out=rows_of(out_0, n)[:, :, 0 : HD - ROPE], in_=pooled[:, :, 0 : HD - ROPE]
            )
            pooled_of[n] = pooled

        def rotate_products(n):
            b, first, size = groups[n]
            products = work.tile([P, size, 2, ROPE], F32)
            nc.gpsimd.tensor_tensor(
                out=products[:],
                in0=pooled_of[n][:, :, HD - ROPE : HD].unsqueeze(2).to_broadcast([P, size, 2, ROPE]),
                in1=table_of[0][:, first : first + size].rearrange("p w o j i -> p w o (j i)"),
                op=ALU.mult,
            )
            products_rope_of[n] = products

        def rotate_sums(n):
            rotated = work.tile([P, groups[n][2], ROPE], F32)
            pairs = products_rope_of[n][:].rearrange("p w o (j i) -> p w o j i", i=2)
            nc.gpsimd.tensor_tensor(
                out=rotated[:].rearrange("p w (j o) -> p w o j", o=2),
                in0=pairs[:, :, :, :, 0],
                in1=pairs[:, :, :, :, 1],
                op=ALU.add,
            )
            nc.sync.dma_start(out=rows_of(out_0, n)[:, :, HD - ROPE : HD], in_=rotated[:])

        def group_due(step):
            for n, (b, first, size) in enumerate(groups):
                if step == b * WPP + first + size:
                    return n
            return None

        for g in range(1, LOADS_AHEAD - FLIPS_AHEAD):
            load(g)
        for step in range(-FLIPS_AHEAD, UNITS + 2 * GROUP + 1):
            due = [group_due(step - k) for k in range(2 * GROUP + 1)]
            if step + LOADS_AHEAD < UNITS:
                load(step + LOADS_AHEAD)
            if due[2] is not None:
                exponentiate(due[2])
            if due[4] is not None:
                fetch_flipped(due[4], 0)
            if due[5] is not None:
                fetch_flipped(due[5], 1)
            if step + FLIPS_AHEAD < UNITS:
                flip_words(step + FLIPS_AHEAD)
            if due[1] is not None:
                top_of_1(due[1])
            if 0 <= step + 1 < UNITS:
                quantise(step + 1)
                project(step + 1)
            if 0 <= step < UNITS:
                land(step)
            if due[0] is not None:
                top_of_4(due[0])
            if due[7] is not None:
                invert(due[7])
            if due[8] is not None:
                rotate_products(due[8])
            if due[3] is not None:
                weigh(due[3])
            if due[1] is not None:
                subtract_top(due[1])
            if due[0] is not None:
                top_of_2(due[0])
            if due[7] is not None:
                divide(due[7])
            if due[8] is not None:
                rotate_sums(due[8])
            if step == 0:
                table_of[0] = rope_table(nc, const, rest)
            if 0 <= step - 1 < UNITS and (step - 1) % WPP == 0:
                move_down((step - 1) // WPP)
            if 0 <= step - 2 < UNITS and (step - 2) % WPP == 0:
                take_moved((step - 2) // WPP)
            if due[3] is not None:
                add_slots(due[3], 0)
            if due[4] is not None:
                add_slots(due[4], 1)
            if due[5] is not None:
                turn_back(due[5], 0)
            if due[6] is not None:
                turn_back(due[6], 1)
